import numpy as np
import ml_dtypes


def mxq(x, axis, fmt="e4m3"):
    dtype, down = {"e4m3": (ml_dtypes.float8_e4m3fn, 7), "e5m2": (ml_dtypes.float8_e5m2, 14)}[fmt]
    v = np.moveaxis(np.asarray(x, np.float32).astype(ml_dtypes.bfloat16).astype(np.float64), axis, -1)
    blocks = v.reshape(v.shape[:-1] + (-1, 32))
    amax = np.abs(blocks).max(-1, keepdims=True)
    byte = np.maximum(np.where(amax > 0, np.frexp(amax)[1] - 1 + 127, 0) - down, 1)
    scale = np.exp2(byte - 127.0)
    codes = (blocks / scale).astype(np.float32).astype(dtype).astype(np.float64)
    return np.moveaxis((codes * scale).reshape(v.shape), -1, axis)


WIDE = False


def mx_kscale(k):
    if not WIDE:
        return np.ones(k)
    levels = np.array([10, -10, 5, -5, 0])
    a = np.random.permutation(np.resize(levels, k // 512 * 4)).reshape(k // 512, 4)
    idx = np.arange(k)
    return np.exp2(a[idx // 512, idx % 128 // 32])


BF16 = ml_dtypes.bfloat16


def bf(x):
    return np.asarray(x, np.float32).astype(BF16)


def f64(x):
    return np.asarray(x).astype(np.float64)


N, DEG, A, B, H = 8, 32, 8192, 256, 512


def setup_inputs():
    s, t = mx_kscale(A), mx_kscale(H)
    return {
        "src_h": bf(np.random.standard_normal((N, DEG, A)) * s),
        "he": bf(np.random.standard_normal((N, DEG, B))),
        "Wcf_w": bf(np.random.standard_normal((H, A)) / np.sqrt(A) / s[None, :]),
        "Wcf_b": bf(np.random.standard_normal(H) * 0.3),
        "Wdf_w": bf(np.random.standard_normal((H, B)) / np.sqrt(B) * t[:, None]),
        "Wdf_b": bf(np.random.standard_normal(H) * 0.3 * t),
        "Wfc_w": bf(np.random.standard_normal((A, H)) * 0.8 / np.sqrt(H) / t[None, :]),
        "Wfc_b": bf(np.random.standard_normal(A) * 0.2),
    }


def reference(src_h, he, Wcf_w, Wcf_b, Wdf_w, Wdf_b, Wfc_w, Wfc_b):
    h_w = (mxq(f64(src_h), 2, "e4m3") @ mxq(f64(Wcf_w), 1, "e4m3").T) + f64(Wcf_b)
    e_vw = f64(he) @ f64(Wdf_w).T + f64(Wdf_b)
    h = h_w * e_vw
    h = (mxq(h, 2, "e4m3") @ mxq(f64(Wfc_w), 1, "e4m3").T) + f64(Wfc_b)
    return np.sum(np.tanh(h), axis=1)

@@ -1,0 +1,274 @@
+from contextlib import ExitStack
+
+import concourse.mybir as mybir
+from concourse.masks import make_identity
+
+F32 = mybir.dt.float32
+BF16 = mybir.dt.bfloat16
+U32 = mybir.dt.uint32
+U8 = mybir.dt.uint8
+FP8X4 = mybir.dt.float8_e4m3fn_x4
+
+P = 128
+NODES, DEG, ATOMS, BOND, HIDDEN = 8, 32, 8192, 256, 512
+TOKENS = NODES * DEG
+TOKEN_TILES = TOKENS // P
+HIDDEN_TILES = HIDDEN // P
+ATOM_TILES = ATOMS // P
+BOND_TILES = BOND // P
+K_PASS = 4 * P
+PASS_WORDS = K_PASS // 2
+BANK = 512
+
+PIECE = 4096
+PIECE_WORDS = PIECE // 2
+PIECE_BANKS = PIECE_WORDS // BANK
+PIECE_CODES = PIECE // 4
+SRC_PIECES = TOKENS * ATOMS // (P * PIECE)
+WCF_PIECES = HIDDEN * ATOMS // (P * PIECE)
+WFC_PIECES = ATOMS * HIDDEN // (P * PIECE)
+PIECES = SRC_PIECES + WCF_PIECES + WFC_PIECES
+SRC_PASSES = PIECE // (TOKEN_TILES * K_PASS)
+W_PASSES = PIECE // K_PASS
+RAW_BUFS = 12
+
+FLOPS = 2 * TOKENS * (ATOMS * HIDDEN + BOND * HIDDEN + HIDDEN * ATOMS)
+
+
+def tile_dtnnmsg_k_kernel(tc, src_h, he, Wcf_w, Wcf_b, Wdf_w, Wdf_b, Wfc_w, Wfc_b, out):
+    nc = tc.nc
+    add, mult = mybir.AluOpType.add, mybir.AluOpType.mult
+    tanh = mybir.ActivationFunctionType.Tanh
+
+    with ExitStack() as ctx:
+        ctx.enter_context(tc.manual_schedule())
+        keep = ctx.enter_context(tc.tile_pool(name="keep", bufs=1))
+        raw_pool = ctx.enter_context(tc.tile_pool(name="raw", bufs=RAW_BUFS))
+        grouped_pool = ctx.enter_context(tc.tile_pool(name="grouped", bufs=3))
+        codes_pool = ctx.enter_context(tc.tile_pool(name="codes", bufs=4))
+        tanh_pool = ctx.enter_context(tc.tile_pool(name="tanh", bufs=4))
+        flip_pool = ctx.enter_context(tc.psum_pool(name="flip", bufs=4))
+        sum_pool = ctx.enter_context(tc.psum_pool(name="sum", bufs=4))
+
+        src_rows = src_h.rearrange("(r x) d a -> (x d) r a", r=TOKEN_TILES)
+        he_rows = he.rearrange("(r x) d b -> (x d) r b", r=TOKEN_TILES)
+        wcf_rows = Wcf_w.rearrange("(u p e) a -> u e p a", u=2, e=2)
+        wdf_rows = Wdf_w.rearrange("(u p e) b -> p u (e b)", u=2, e=2)
+        wfc_rows = Wfc_w.rearrange("(p j) h -> p j h", j=ATOM_TILES)
+
+        def load_piece(i):
+            raw = raw_pool.tile([P, PIECE], BF16, tag="raw")
+            if i < SRC_PIECES:
+                atoms = slice(i * SRC_PASSES * K_PASS, (i + 1) * SRC_PASSES * K_PASS)
+                nc.sync.dma_start(
+                    out=raw[:].rearrange("p (r a) -> p r a", r=TOKEN_TILES), in_=src_rows[:, :, atoms]
+                )
+            elif i < SRC_PIECES + WCF_PIECES:
+                t, half = divmod(i - SRC_PIECES, 2)
+                nc.sync.dma_start(
+                    out=raw[:], in_=wcf_rows[t // 2, t % 2, :, half * PIECE : (half + 1) * PIECE]
+                )
+            else:
+                first = (i - SRC_PIECES - WCF_PIECES) * W_PASSES
+                nc.sync.dma_start(
+                    out=raw[:].rearrange("p (j h) -> p j h", j=W_PASSES),
+                    in_=wfc_rows[:, first : first + W_PASSES, :],
+                )
+            return raw
+
+        he_sb = keep.tile([P, TOKEN_TILES * BOND], BF16)
+        nc.scalar.dma_start(out=he_sb[:].rearrange("p (r b) -> p r b", r=TOKEN_TILES), in_=he_rows)
+        wdf_sb = keep.tile([P, HIDDEN_TILES * BOND], BF16)
+        nc.scalar.dma_start(out=wdf_sb[:].rearrange("p (u x) -> p u x", u=2), in_=wdf_rows)
+        wcf_b_bf = keep.tile([P, HIDDEN_TILES], BF16)
+        nc.scalar.dma_start(
+            out=wcf_b_bf[:].rearrange("p (u e) -> p u e", u=2),
+            in_=Wcf_b.rearrange("(u p e) -> p u e", u=2, e=2),
+        )
+        wdf_b_bf = keep.tile([P, HIDDEN_TILES], BF16)
+        nc.scalar.dma_start(
+            out=wdf_b_bf[:].rearrange("p (u e) -> p u e", u=2),
+            in_=Wdf_b.rearrange("(u p e) -> p u e", u=2, e=2),
+        )
+        wfc_b_bf = keep.tile([P, ATOM_TILES], BF16)
+        nc.scalar.dma_start(out=wfc_b_bf[:], in_=Wfc_b.rearrange("(p j) -> p j", j=ATOM_TILES))
+
+        raws = [load_piece(i) for i in range(RAW_BUFS)]
+
+        ident_f32 = keep.tile([P, P], F32)
+        make_identity(nc, ident_f32[:])
+        ident_bf = keep.tile([P, P], BF16)
+        make_identity(nc, ident_bf[:])
+
+        warm = keep.tile([P, 2], F32)
+        nc.vector.memset(warm[:], 0.0)
+        nc.scalar.activation(out=warm[:, 1:2], in_=warm[:, 0:1], func=tanh)
+
+        wcf_b = keep.tile([P, HIDDEN_TILES], F32)
+        nc.vector.tensor_copy(out=wcf_b[:], in_=wcf_b_bf[:])
+        wdf_b = keep.tile([P, HIDDEN_TILES], F32)
+        nc.vector.tensor_copy(out=wdf_b[:], in_=wdf_b_bf[:])
+        wfc_b = keep.tile([P, ATOM_TILES], F32)
+        nc.vector.tensor_copy(out=wfc_b[:], in_=wfc_b_bf[:])
+
+        wdf_flip = flip_pool.tile([P, BOND_TILES * HIDDEN], BF16, tag="flip")
+        for kb in range(BOND_TILES):
+            for t in range(HIDDEN_TILES):
+                nc.tensor.transpose(
+                    wdf_flip[:, (kb * HIDDEN_TILES + t) * P : (kb * HIDDEN_TILES + t + 1) * P],
+                    wdf_sb[:, t * BOND + kb * P : t * BOND + (kb + 1) * P],
+                    ident_bf[:],
+                )
+        wdf_t = keep.tile([P, BOND_TILES * HIDDEN], BF16)
+        nc.vector.tensor_copy(out=wdf_t[:], in_=wdf_flip[:])
+        he_flip = flip_pool.tile([P, BOND_TILES * TOKENS], BF16, tag="flip")
+        for kb in range(BOND_TILES):
+            for r in range(TOKEN_TILES):
+                nc.tensor.transpose(
+                    he_flip[:, (kb * TOKEN_TILES + r) * P : (kb * TOKEN_TILES + r + 1) * P],
+                    he_sb[:, r * BOND + kb * P : r * BOND + (kb + 1) * P],
+                    ident_bf[:],
+                )
+        he_t = keep.tile([P, BOND_TILES * TOKENS], BF16)
+        nc.scalar.copy(out=he_t[:], in_=he_flip[:])
+        e_vw = keep.tile([P, HIDDEN_TILES * TOKENS], F32)
+        for t in range(HIDDEN_TILES):
+            e_sum = sum_pool.tile([P, TOKENS], F32, tag="sum")
+            for kb in range(BOND_TILES):
+                nc.tensor.matmul(
+                    e_sum[:],
+                    lhsT=wdf_t[:, (kb * HIDDEN_TILES + t) * P : (kb * HIDDEN_TILES + t + 1) * P],
+                    rhs=he_t[:, kb * TOKENS : (kb + 1) * TOKENS],
+                    start=(kb == 0),
+                    stop=(kb == BOND_TILES - 1),
+                )
+            nc.vector.tensor_scalar_add(
+                out=e_vw[:, t * TOKENS : (t + 1) * TOKENS], in0=e_sum[:], scalar1=wdf_b[:, t : t + 1]
+            )
+
+        src_codes = [
+            keep.tile([P, PIECE_CODES], U32, name="src_codes%d" % c, align_bytes=64)
+            for c in range(SRC_PIECES)
+        ]
+        src_scales = [
+            keep.tile([P, PIECE_CODES], U8, name="src_scales%d" % c, align_bytes=64)
+            for c in range(SRC_PIECES)
+        ]
+        h_grouped = keep.tile([P, TOKENS, HIDDEN_TILES], BF16, align_bytes=64)
+        h_codes = keep.tile([P, TOKENS], U32, align_bytes=64)
+        h_scales = keep.tile([P, TOKENS], U8, align_bytes=64)
+        sums = keep.tile([P, NODES, ATOM_TILES], F32)
+
+        def transpose_and_regroup(raw, row_tiles):
+            bank_passes = BANK // (2 * P * row_tiles)
+            words = raw[:].bitcast(F32).rearrange("p (r g u w) -> p r g u w", r=row_tiles, u=2, w=P)
+            grouped = grouped_pool.tile([P, PIECE], BF16, tag="grouped", align_bytes=64)
+            grouped_words = grouped[:].bitcast(F32)
+            for b in range(PIECE_BANKS):
+                flip = flip_pool.tile([P, BANK], F32, tag="flip")
+                blocks = flip[:].rearrange("p (g u r w) -> p g u r w", g=bank_passes, u=2, r=row_tiles)
+                for g in range(bank_passes):
+                    for u in range(2):
+                        for r in range(row_tiles):
+                            nc.tensor.transpose(
+                                blocks[:, g, u, r, :], words[:, r, b * bank_passes + g, u, :], ident_f32[:]
+                            )
+                pairs_in = flip[:].rearrange("p (g u c) -> p g c u", g=bank_passes, u=2)
+                pairs_out = grouped_words[:, b * BANK : (b + 1) * BANK].rearrange(
+                    "p (g c u) -> p g c u", g=bank_passes, u=2
+                )
+                if b < PIECE_BANKS - 1:
+                    nc.scalar.copy(out=pairs_out, in_=pairs_in)
+                else:
+                    nc.vector.tensor_copy(out=pairs_out, in_=pairs_in)
+            return grouped
+
+        def quantise(grouped, codes, scales):
+            nc.vector.quantize_mx(out=codes[:].bitcast(FP8X4), scales=scales[:], in_=grouped[:])
+
+        def hidden_passes(t, half, h_w, codes, scales):
+            for a in range(W_PASSES):
+                g = half * W_PASSES + a
+                c, s = divmod(g, SRC_PASSES)
+                nc.tensor.matmul_mx(
+                    out=h_w[:],
+                    lhsT=codes[:, a * P : (a + 1) * P].bitcast(FP8X4),
+                    lhsT_scale=scales[:, a * P : (a + 1) * P],
+                    rhs=src_codes[c][:, s * TOKENS : (s + 1) * TOKENS].bitcast(FP8X4),
+                    rhs_scale=src_scales[c][:, s * TOKENS : (s + 1) * TOKENS],
+                    start=(g == 0),
+                    stop=(g == ATOMS // K_PASS - 1),
+                )
+
+        def messages(first_tile, codes, scales):
+            for b in range(W_PASSES // 2):
+                z = sum_pool.tile([P, 2 * TOKENS], F32, tag="sum")
+                for s in range(2):
+                    a = 2 * b + s
+                    nc.tensor.matmul_mx(
+                        out=z[:, s * TOKENS : (s + 1) * TOKENS],
+                        lhsT=codes[:, a * P : (a + 1) * P].bitcast(FP8X4),
+                        lhsT_scale=scales[:, a * P : (a + 1) * P],
+                        rhs=h_codes[:].bitcast(FP8X4),
+                        rhs_scale=h_scales[:],
+                        start=True,
+                        stop=True,
+                    )
+                j = first_tile + 2 * b
+                tanh_z = tanh_pool.tile([P, 2 * TOKENS], F32, tag="tanh")
+                for s in range(2):
+                    nc.scalar.activation(
+                        out=tanh_z[:, s * TOKENS : (s + 1) * TOKENS],
+                        in_=z[:, s * TOKENS : (s + 1) * TOKENS],
+                        func=tanh,
+                        bias=wfc_b[:, j + s : j + s + 1],
+                    )
+                nc.vector.tensor_reduce(
+                    out=sums[:, :, j : j + 2].rearrange("p n j -> p j n"),
+                    in_=tanh_z[:].rearrange("p (j n d) -> p j n d", j=2, n=NODES),
+                    axis=mybir.AxisListType.X,
+                    op=add,
+                )
+
+        grouped_of, codes_of, scales_of = {}, {}, {}
+        h_w = None
+        for i in range(PIECES + 2):
+            q = i - 1
+            if 0 <= q < PIECES:
+                if q < SRC_PIECES:
+                    codes_of[q], scales_of[q] = src_codes[q], src_scales[q]
+                else:
+                    codes_of[q] = codes_pool.tile([P, PIECE_CODES], U32, name="codes", align_bytes=64)
+                    scales_of[q] = codes_pool.tile([P, PIECE_CODES], U8, name="scales", align_bytes=64)
+                quantise(grouped_of[q], codes_of[q], scales_of[q])
+
+            if i < PIECES:
+                grouped_of[i] = transpose_and_regroup(raws[i], TOKEN_TILES if i < SRC_PIECES else 1)
+                if i + RAW_BUFS < PIECES:
+                    raws.append(load_piece(i + RAW_BUFS))
+
+            m = i - 2
+            if SRC_PIECES <= m < SRC_PIECES + WCF_PIECES:
+                t, half = divmod(m - SRC_PIECES, 2)
+                if half == 0:
+                    h_w = sum_pool.tile([P, TOKENS], F32, tag="sum")
+                hidden_passes(t, half, h_w, codes_of[m], scales_of[m])
+                if half == 1:
+                    nc.vector.scalar_tensor_tensor(
+                        out=h_grouped[:, :, t],
+                        in0=h_w[:],
+                        scalar=wcf_b[:, t : t + 1],
+                        in1=e_vw[:, t * TOKENS : (t + 1) * TOKENS],
+                        op0=add,
+                        op1=mult,
+                    )
+                if m == SRC_PIECES + WCF_PIECES - 1:
+                    nc.vector.quantize_mx(
+                        out=h_codes[:].bitcast(FP8X4),
+                        scales=h_scales[:],
+                        in_=h_grouped[:].rearrange("p c t -> p (c t)"),
+                    )
+            elif SRC_PIECES + WCF_PIECES <= m < PIECES:
+                messages((m - SRC_PIECES - WCF_PIECES) * W_PASSES, codes_of[m], scales_of[m])
+
+        nc.sync.dma_start(out=out.rearrange("n (p j) -> p n j", j=ATOM_TILES), in_=sums[:])

@@ -41,7 +41,6 @@ def tile_dtnnmsg_k_kernel(tc, src_h, he, Wcf_w, Wcf_b, Wdf_w, Wdf_b, Wfc_w, Wfc_
     tanh = mybir.ActivationFunctionType.Tanh
 
     with ExitStack() as ctx:
-        ctx.enter_context(tc.manual_schedule())
         keep = ctx.enter_context(tc.tile_pool(name="keep", bufs=1))
         raw_pool = ctx.enter_context(tc.tile_pool(name="raw", bufs=RAW_BUFS))
         grouped_pool = ctx.enter_context(tc.tile_pool(name="grouped", bufs=3))

@@ -24,13 +24,19 @@ PIECE = 4096
 PIECE_WORDS = PIECE // 2
 PIECE_BANKS = PIECE_WORDS // BANK
 PIECE_CODES = PIECE // 4
-SRC_PIECES = TOKENS * ATOMS // (P * PIECE)
-WCF_PIECES = HIDDEN * ATOMS // (P * PIECE)
-WFC_PIECES = ATOMS * HIDDEN // (P * PIECE)
-PIECES = SRC_PIECES + WCF_PIECES + WFC_PIECES
-SRC_PASSES = PIECE // (TOKEN_TILES * K_PASS)
-W_PASSES = PIECE // K_PASS
-RAW_BUFS = 12
+CHUNK_TILES = 2
+CHUNK_PASSES = PIECE // (CHUNK_TILES * K_PASS)
+CHUNK_ATOMS = CHUNK_PASSES * K_PASS
+CHUNKS = ATOMS // CHUNK_ATOMS
+CHUNK_PIECES = 1 + HIDDEN_TILES // CHUNK_TILES
+WFC_TILES = PIECE // HIDDEN
+WFC_PIECES = ATOM_TILES // WFC_TILES
+FIRST_WFC = CHUNKS * CHUNK_PIECES
+PIECES = FIRST_WFC + WFC_PIECES
+RAW_BUFS = 11
+GROUP_TILES = P // NODES
+GROUP_PIECES = GROUP_TILES // WFC_TILES
+HALF_DEG = DEG // 2
 
 FLOPS = 2 * TOKENS * (ATOMS * HIDDEN + BOND * HIDDEN + HIDDEN * ATOMS)
 
@@ -45,40 +51,39 @@ def tile_dtnnmsg_k_kernel(tc, src_h, he, Wcf_w, Wcf_b, Wdf_w, Wdf_b, Wfc_w, Wfc_
         raw_pool = ctx.enter_context(tc.tile_pool(name="raw", bufs=RAW_BUFS))
         grouped_pool = ctx.enter_context(tc.tile_pool(name="grouped", bufs=3))
         codes_pool = ctx.enter_context(tc.tile_pool(name="codes", bufs=4))
-        tanh_pool = ctx.enter_context(tc.tile_pool(name="tanh", bufs=4))
+        tanh_pool = ctx.enter_context(tc.tile_pool(name="tanh", bufs=3))
+        store_pool = ctx.enter_context(tc.tile_pool(name="store", bufs=2))
         flip_pool = ctx.enter_context(tc.psum_pool(name="flip", bufs=4))
         sum_pool = ctx.enter_context(tc.psum_pool(name="sum", bufs=4))
 
         src_rows = src_h.rearrange("(r x) d a -> (x d) r a", r=TOKEN_TILES)
         he_rows = he.rearrange("(r x) d b -> (x d) r b", r=TOKEN_TILES)
-        wcf_rows = Wcf_w.rearrange("(u p e) a -> u e p a", u=2, e=2)
+        wcf_rows = Wcf_w.rearrange("(u p e) a -> u p e a", u=2, e=2)
         wdf_rows = Wdf_w.rearrange("(u p e) b -> p u (e b)", u=2, e=2)
-        wfc_rows = Wfc_w.rearrange("(p j) h -> p j h", j=ATOM_TILES)
+        wfc_rows = Wfc_w.rearrange("(j p) h -> p j h", p=P)
+        out_tiles = out.rearrange("n (g j p) -> g n j p", j=GROUP_TILES, p=P)
 
         def load_piece(i):
             raw = raw_pool.tile([P, PIECE], BF16, tag="raw")
-            if i < SRC_PIECES:
-                atoms = slice(i * SRC_PASSES * K_PASS, (i + 1) * SRC_PASSES * K_PASS)
+            if i < FIRST_WFC:
+                c, part = divmod(i, CHUNK_PIECES)
+                rows = src_rows if part == 0 else wcf_rows[part - 1]
                 nc.sync.dma_start(
-                    out=raw[:].rearrange("p (r a) -> p r a", r=TOKEN_TILES), in_=src_rows[:, :, atoms]
-                )
-            elif i < SRC_PIECES + WCF_PIECES:
-                t, half = divmod(i - SRC_PIECES, 2)
-                nc.sync.dma_start(
-                    out=raw[:], in_=wcf_rows[t // 2, t % 2, :, half * PIECE : (half + 1) * PIECE]
+                    out=raw[:].rearrange("p (r a) -> p r a", r=CHUNK_TILES),
+                    in_=rows[:, :, c * CHUNK_ATOMS : (c + 1) * CHUNK_ATOMS],
                 )
             else:
-                first = (i - SRC_PIECES - WCF_PIECES) * W_PASSES
+                first = (i - FIRST_WFC) * WFC_TILES
                 nc.sync.dma_start(
-                    out=raw[:].rearrange("p (j h) -> p j h", j=W_PASSES),
-                    in_=wfc_rows[:, first : first + W_PASSES, :],
+                    out=raw[:].rearrange("p (j h) -> p j h", j=WFC_TILES),
+                    in_=wfc_rows[:, first : first + WFC_TILES, :],
                 )
             return raw
 
         he_sb = keep.tile([P, TOKEN_TILES * BOND], BF16)
-        nc.scalar.dma_start(out=he_sb[:].rearrange("p (r b) -> p r b", r=TOKEN_TILES), in_=he_rows)
+        nc.sync.dma_start(out=he_sb[:].rearrange("p (r b) -> p r b", r=TOKEN_TILES), in_=he_rows)
         wdf_sb = keep.tile([P, HIDDEN_TILES * BOND], BF16)
-        nc.scalar.dma_start(out=wdf_sb[:].rearrange("p (u x) -> p u x", u=2), in_=wdf_rows)
+        nc.sync.dma_start(out=wdf_sb[:].rearrange("p (u x) -> p u x", u=2), in_=wdf_rows)
         wcf_b_bf = keep.tile([P, HIDDEN_TILES], BF16)
         nc.scalar.dma_start(
             out=wcf_b_bf[:].rearrange("p (u e) -> p u e", u=2),
@@ -89,8 +94,9 @@ def tile_dtnnmsg_k_kernel(tc, src_h, he, Wcf_w, Wcf_b, Wdf_w, Wdf_b, Wfc_w, Wfc_
             out=wdf_b_bf[:].rearrange("p (u e) -> p u e", u=2),
             in_=Wdf_b.rearrange("(u p e) -> p u e", u=2, e=2),
         )
-        wfc_b_bf = keep.tile([P, ATOM_TILES], BF16)
-        nc.scalar.dma_start(out=wfc_b_bf[:], in_=Wfc_b.rearrange("(p j) -> p j", j=ATOM_TILES))
+        wfc_b_rows = keep.tile([P, P], BF16)
+        nc.vector.memset(wfc_b_rows[:], 0.0)
+        nc.scalar.dma_start(out=wfc_b_rows[:ATOM_TILES, :], in_=Wfc_b.rearrange("(j p) -> j p", p=P))
 
         raws = [load_piece(i) for i in range(RAW_BUFS)]
 
@@ -107,8 +113,6 @@ def tile_dtnnmsg_k_kernel(tc, src_h, he, Wcf_w, Wcf_b, Wdf_w, Wdf_b, Wfc_w, Wfc_
         nc.vector.tensor_copy(out=wcf_b[:], in_=wcf_b_bf[:])
         wdf_b = keep.tile([P, HIDDEN_TILES], F32)
         nc.vector.tensor_copy(out=wdf_b[:], in_=wdf_b_bf[:])
-        wfc_b = keep.tile([P, ATOM_TILES], F32)
-        nc.vector.tensor_copy(out=wfc_b[:], in_=wfc_b_bf[:])
 
         wdf_flip = flip_pool.tile([P, BOND_TILES * HIDDEN], BF16, tag="flip")
         for kb in range(BOND_TILES):
@@ -145,20 +149,24 @@ def tile_dtnnmsg_k_kernel(tc, src_h, he, Wcf_w, Wcf_b, Wdf_w, Wdf_b, Wfc_w, Wfc_
                 out=e_vw[:, t * TOKENS : (t + 1) * TOKENS], in0=e_sum[:], scalar1=wdf_b[:, t : t + 1]
             )
 
+        wfc_b_flip = flip_pool.tile([P, P], BF16, tag="flip")
+        nc.tensor.transpose(wfc_b_flip[:], wfc_b_rows[:], ident_bf[:])
+        wfc_b = keep.tile([P, ATOM_TILES], F32)
+        nc.vector.tensor_copy(out=wfc_b[:], in_=wfc_b_flip[:, :ATOM_TILES])
+
         src_codes = [
             keep.tile([P, PIECE_CODES], U32, name="src_codes%d" % c, align_bytes=64)
-            for c in range(SRC_PIECES)
+            for c in range(CHUNKS)
         ]
         src_scales = [
             keep.tile([P, PIECE_CODES], U8, name="src_scales%d" % c, align_bytes=64)
-            for c in range(SRC_PIECES)
+            for c in range(CHUNKS)
         ]
         h_grouped = keep.tile([P, TOKENS, HIDDEN_TILES], BF16, align_bytes=64)
         h_codes = keep.tile([P, TOKENS], U32, align_bytes=64)
         h_scales = keep.tile([P, TOKENS], U8, align_bytes=64)
-        sums = keep.tile([P, NODES, ATOM_TILES], F32)
 
-        def transpose_and_regroup(raw, row_tiles):
+        def transpose_and_regroup(raw, row_tiles, scalar_banks):
             bank_passes = BANK // (2 * P * row_tiles)
             words = raw[:].bitcast(F32).rearrange("p (r g u w) -> p r g u w", r=row_tiles, u=2, w=P)
             grouped = grouped_pool.tile([P, PIECE], BF16, tag="grouped", align_bytes=64)
@@ -176,7 +184,7 @@ def tile_dtnnmsg_k_kernel(tc, src_h, he, Wcf_w, Wcf_b, Wdf_w, Wdf_b, Wfc_w, Wfc_
                 pairs_out = grouped_words[:, b * BANK : (b + 1) * BANK].rearrange(
                     "p (g c u) -> p g c u", g=bank_passes, u=2
                 )
-                if b < PIECE_BANKS - 1:
+                if b in scalar_banks:
                     nc.scalar.copy(out=pairs_out, in_=pairs_in)
                 else:
                     nc.vector.tensor_copy(out=pairs_out, in_=pairs_in)
@@ -185,22 +193,32 @@ def tile_dtnnmsg_k_kernel(tc, src_h, he, Wcf_w, Wcf_b, Wdf_w, Wdf_b, Wfc_w, Wfc_
         def quantise(grouped, codes, scales):
             nc.vector.quantize_mx(out=codes[:].bitcast(FP8X4), scales=scales[:], in_=grouped[:])
 
-        def hidden_passes(t, half, h_w, codes, scales):
-            for a in range(W_PASSES):
-                g = half * W_PASSES + a
-                c, s = divmod(g, SRC_PASSES)
-                nc.tensor.matmul_mx(
-                    out=h_w[:],
-                    lhsT=codes[:, a * P : (a + 1) * P].bitcast(FP8X4),
-                    lhsT_scale=scales[:, a * P : (a + 1) * P],
-                    rhs=src_codes[c][:, s * TOKENS : (s + 1) * TOKENS].bitcast(FP8X4),
-                    rhs_scale=src_scales[c][:, s * TOKENS : (s + 1) * TOKENS],
-                    start=(g == 0),
-                    stop=(g == ATOMS // K_PASS - 1),
-                )
+        def hidden_passes(c, u, h_w, codes, scales):
+            for e in range(CHUNK_TILES):
+                for s in range(CHUNK_PASSES):
+                    rows = slice((CHUNK_TILES * s + e) * P, (CHUNK_TILES * s + e + 1) * P)
+                    nc.tensor.matmul_mx(
+                        out=h_w[CHUNK_TILES * u + e][:],
+                        lhsT=codes[:, rows].bitcast(FP8X4),
+                        lhsT_scale=scales[:, rows],
+                        rhs=src_codes[c][:, s * TOKENS : (s + 1) * TOKENS].bitcast(FP8X4),
+                        rhs_scale=src_scales[c][:, s * TOKENS : (s + 1) * TOKENS],
+                        start=(c == 0 and s == 0),
+                        stop=(c == CHUNKS - 1 and s == CHUNK_PASSES - 1),
+                    )
 
-        def messages(first_tile, codes, scales):
-            for b in range(W_PASSES // 2):
+        def hidden_product(t, h_w):
+            nc.vector.scalar_tensor_tensor(
+                out=h_grouped[:, :, t].rearrange("p (d n) -> p d n", n=NODES),
+                in0=h_w[t][:].rearrange("p (n d) -> p d n", n=NODES),
+                scalar=wcf_b[:, t : t + 1],
+                in1=e_vw[:, t * TOKENS : (t + 1) * TOKENS].rearrange("p (n d) -> p d n", n=NODES),
+                op0=add,
+                op1=mult,
+            )
+
+        def messages(w, codes, scales, tanh_z):
+            for b in range(WFC_TILES // 2):
                 z = sum_pool.tile([P, 2 * TOKENS], F32, tag="sum")
                 for s in range(2):
                     a = 2 * b + s
@@ -213,61 +231,88 @@ def tile_dtnnmsg_k_kernel(tc, src_h, he, Wcf_w, Wcf_b, Wdf_w, Wdf_b, Wfc_w, Wfc_
                         start=True,
                         stop=True,
                     )
-                j = first_tile + 2 * b
-                tanh_z = tanh_pool.tile([P, 2 * TOKENS], F32, tag="tanh")
                 for s in range(2):
+                    a = 2 * b + s
+                    j = w * WFC_TILES + a
                     nc.scalar.activation(
-                        out=tanh_z[:, s * TOKENS : (s + 1) * TOKENS],
-                        in_=z[:, s * TOKENS : (s + 1) * TOKENS],
+                        out=tanh_z[:, :, j % GROUP_TILES, :],
+                        in_=z[:, s * TOKENS : (s + 1) * TOKENS].rearrange("p (d n) -> p d n", n=NODES),
                         func=tanh,
-                        bias=wfc_b[:, j + s : j + s + 1],
+                        bias=wfc_b[:, j : j + 1],
                     )
-                nc.vector.tensor_reduce(
-                    out=sums[:, :, j : j + 2].rearrange("p n j -> p j n"),
-                    in_=tanh_z[:].rearrange("p (j n d) -> p j n d", j=2, n=NODES),
-                    axis=mybir.AxisListType.X,
-                    op=add,
-                )
 
-        grouped_of, codes_of, scales_of = {}, {}, {}
-        h_w = None
-        for i in range(PIECES + 2):
+        def add_halves(w, tanh_z):
+            first = (w % GROUP_PIECES) * WFC_TILES
+            low = tanh_z[:, :HALF_DEG, first : first + WFC_TILES, :]
+            nc.vector.tensor_add(out=low, in0=low, in1=tanh_z[:, HALF_DEG:, first : first + WFC_TILES, :])
+
+        def sum_and_store(group, tanh_z):
+            total = flip_pool.tile([P, P], F32, tag="flip")
+            for dd in range(HALF_DEG):
+                nc.tensor.matmul(
+                    total[:],
+                    lhsT=tanh_z[:, dd, :, :].rearrange("p j n -> p (j n)"),
+                    rhs=ident_f32[:],
+                    is_transpose=True,
+                    start=(dd == 0),
+                    stop=(dd == HALF_DEG - 1),
+                )
+            rows = store_pool.tile([P, P], F32, tag="rows")
+            nc.vector.tensor_copy(out=rows[:], in_=total[:])
+            for n in range(NODES):
+                nc.sync.dma_start(out=out_tiles[group, n], in_=rows[n::NODES, :])
+
+        ctx.enter_context(tc.manual_schedule())
+        grouped_of, codes_of, scales_of, tanh_of, h_w = {}, {}, {}, {}, {}
+        for i in range(PIECES + 4):
             q = i - 1
             if 0 <= q < PIECES:
-                if q < SRC_PIECES:
-                    codes_of[q], scales_of[q] = src_codes[q], src_scales[q]
+                if q < FIRST_WFC and q % CHUNK_PIECES == 0:
+                    codes_of[q], scales_of[q] = src_codes[q // CHUNK_PIECES], src_scales[q // CHUNK_PIECES]
                 else:
                     codes_of[q] = codes_pool.tile([P, PIECE_CODES], U32, name="codes", align_bytes=64)
                     scales_of[q] = codes_pool.tile([P, PIECE_CODES], U8, name="scales", align_bytes=64)
                 quantise(grouped_of[q], codes_of[q], scales_of[q])
 
+            w = i - 3 - FIRST_WFC
+            if 0 <= w < WFC_PIECES:
+                add_halves(w, tanh_of[w // GROUP_PIECES])
+
             if i < PIECES:
-                grouped_of[i] = transpose_and_regroup(raws[i], TOKEN_TILES if i < SRC_PIECES else 1)
+                scalar_banks = (0, 2) if i >= FIRST_WFC + 2 else (0, 1, 2)
+                grouped_of[i] = transpose_and_regroup(
+                    raws[i], CHUNK_TILES if i < FIRST_WFC else 1, scalar_banks
+                )
                 if i + RAW_BUFS < PIECES:
                     raws.append(load_piece(i + RAW_BUFS))
 
             m = i - 2
-            if SRC_PIECES <= m < SRC_PIECES + WCF_PIECES:
-                t, half = divmod(m - SRC_PIECES, 2)
-                if half == 0:
-                    h_w = sum_pool.tile([P, TOKENS], F32, tag="sum")
-                hidden_passes(t, half, h_w, codes_of[m], scales_of[m])
-                if half == 1:
-                    nc.vector.scalar_tensor_tensor(
-                        out=h_grouped[:, :, t],
-                        in0=h_w[:],
-                        scalar=wcf_b[:, t : t + 1],
-                        in1=e_vw[:, t * TOKENS : (t + 1) * TOKENS],
-                        op0=add,
-                        op1=mult,
-                    )
-                if m == SRC_PIECES + WCF_PIECES - 1:
+            if 0 <= m < FIRST_WFC:
+                c, part = divmod(m, CHUNK_PIECES)
+                if part > 0:
+                    u = part - 1
+                    pair = range(CHUNK_TILES * u, CHUNK_TILES * u + CHUNK_TILES)
+                    if c == 0:
+                        for t in pair:
+                            h_w[t] = sum_pool.tile([P, TOKENS], F32, name="h_w", tag="sum")
+                    hidden_passes(c, u, h_w, codes_of[m], scales_of[m])
+                    if c == CHUNKS - 1:
+                        for t in pair:
+                            hidden_product(t, h_w)
+                if m == FIRST_WFC - 1:
                     nc.vector.quantize_mx(
                         out=h_codes[:].bitcast(FP8X4),
                         scales=h_scales[:],
                         in_=h_grouped[:].rearrange("p c t -> p (c t)"),
                     )
-            elif SRC_PIECES + WCF_PIECES <= m < PIECES:
-                messages((m - SRC_PIECES - WCF_PIECES) * W_PASSES, codes_of[m], scales_of[m])
+            elif FIRST_WFC <= m < PIECES:
+                w = m - FIRST_WFC
+                if w % GROUP_PIECES == 0:
+                    tanh_of[w // GROUP_PIECES] = tanh_pool.tile(
+                        [P, DEG, GROUP_TILES, NODES], F32, name="tanh_z"
+                    )
+                messages(w, codes_of[m], scales_of[m], tanh_of[w // GROUP_PIECES])
 
-        nc.sync.dma_start(out=out.rearrange("n (p j) -> p n j", j=ATOM_TILES), in_=sums[:])
+            w = i - 4 - FIRST_WFC
+            if w >= 0 and w % GROUP_PIECES == GROUP_PIECES - 1:
+                sum_and_store(w // GROUP_PIECES, tanh_of[w // GROUP_PIECES])

@@ -209,10 +209,10 @@ def tile_dtnnmsg_k_kernel(tc, src_h, he, Wcf_w, Wcf_b, Wdf_w, Wdf_b, Wfc_w, Wfc_
 
         def hidden_product(t, h_w):
             nc.vector.scalar_tensor_tensor(
-                out=h_grouped[:, :, t].rearrange("p (d n) -> p d n", n=NODES),
-                in0=h_w[t][:].rearrange("p (n d) -> p d n", n=NODES),
+                out=h_grouped[:, :, t],
+                in0=h_w[t][:],
                 scalar=wcf_b[:, t : t + 1],
-                in1=e_vw[:, t * TOKENS : (t + 1) * TOKENS].rearrange("p (n d) -> p d n", n=NODES),
+                in1=e_vw[:, t * TOKENS : (t + 1) * TOKENS],
                 op0=add,
                 op1=mult,
             )
@@ -236,7 +236,7 @@ def tile_dtnnmsg_k_kernel(tc, src_h, he, Wcf_w, Wcf_b, Wdf_w, Wdf_b, Wfc_w, Wfc_
                     j = w * WFC_TILES + a
                     nc.scalar.activation(
                         out=tanh_z[:, :, j % GROUP_TILES, :],
-                        in_=z[:, s * TOKENS : (s + 1) * TOKENS].rearrange("p (d n) -> p d n", n=NODES),
+                        in_=z[:, s * TOKENS : (s + 1) * TOKENS].rearrange("p (n d) -> p d n", n=NODES),
                         func=tanh,
                         bias=wfc_b[:, j : j + 1],
                     )

@@ -193,19 +193,18 @@ def tile_dtnnmsg_k_kernel(tc, src_h, he, Wcf_w, Wcf_b, Wdf_w, Wdf_b, Wfc_w, Wfc_
         def quantise(grouped, codes, scales):
             nc.vector.quantize_mx(out=codes[:].bitcast(FP8X4), scales=scales[:], in_=grouped[:])
 
-        def hidden_passes(c, u, h_w, codes, scales):
-            for e in range(CHUNK_TILES):
-                for s in range(CHUNK_PASSES):
-                    rows = slice((CHUNK_TILES * s + e) * P, (CHUNK_TILES * s + e + 1) * P)
-                    nc.tensor.matmul_mx(
-                        out=h_w[CHUNK_TILES * u + e][:],
-                        lhsT=codes[:, rows].bitcast(FP8X4),
-                        lhsT_scale=scales[:, rows],
-                        rhs=src_codes[c][:, s * TOKENS : (s + 1) * TOKENS].bitcast(FP8X4),
-                        rhs_scale=src_scales[c][:, s * TOKENS : (s + 1) * TOKENS],
-                        start=(c == 0 and s == 0),
-                        stop=(c == CHUNKS - 1 and s == CHUNK_PASSES - 1),
-                    )
+        def hidden_pass(c, t, s, h_w, codes, scales):
+            first_row = (CHUNK_TILES * s + t % CHUNK_TILES) * P
+            rows = slice(first_row, first_row + P)
+            nc.tensor.matmul_mx(
+                out=h_w[t][:],
+                lhsT=codes[:, rows].bitcast(FP8X4),
+                lhsT_scale=scales[:, rows],
+                rhs=src_codes[c][:, s * TOKENS : (s + 1) * TOKENS].bitcast(FP8X4),
+                rhs_scale=src_scales[c][:, s * TOKENS : (s + 1) * TOKENS],
+                start=(c == 0 and s == 0),
+                stop=(c == CHUNKS - 1 and s == CHUNK_PASSES - 1),
+            )
 
         def hidden_product(t, h_w):
             nc.vector.scalar_tensor_tensor(
@@ -217,8 +216,8 @@ def tile_dtnnmsg_k_kernel(tc, src_h, he, Wcf_w, Wcf_b, Wdf_w, Wdf_b, Wfc_w, Wfc_
                 op1=mult,
             )
 
-        def messages(w, codes, scales, tanh_z):
-            for b in range(WFC_TILES // 2):
+        def messages(w, banks, codes, scales, tanh_z):
+            for b in banks:
                 z = sum_pool.tile([P, 2 * TOKENS], F32, tag="sum")
                 for s in range(2):
                     a = 2 * b + s
@@ -264,7 +263,15 @@ def tile_dtnnmsg_k_kernel(tc, src_h, he, Wcf_w, Wcf_b, Wdf_w, Wdf_b, Wfc_w, Wfc_
 
         ctx.enter_context(tc.manual_schedule())
         grouped_of, codes_of, scales_of, tanh_of, h_w = {}, {}, {}, {}, {}
-        for i in range(PIECES + 4):
+        passes = [
+            (CHUNK_PIECES * c + 1 + t // CHUNK_TILES, t, s)
+            for c in range(CHUNKS)
+            for t in range(HIDDEN_TILES)
+            for s in range(CHUNK_PASSES)
+        ]
+        chunk_total = HIDDEN_TILES * CHUNK_PASSES
+        done = 0
+        for i in range(PIECES + 5):
             q = i - 1
             if 0 <= q < PIECES:
                 if q < FIRST_WFC and q % CHUNK_PIECES == 0:
@@ -273,10 +280,6 @@ def tile_dtnnmsg_k_kernel(tc, src_h, he, Wcf_w, Wcf_b, Wdf_w, Wdf_b, Wfc_w, Wfc_
                     codes_of[q] = codes_pool.tile([P, PIECE_CODES], U32, name="codes", align_bytes=64)
                     scales_of[q] = codes_pool.tile([P, PIECE_CODES], U8, name="scales", align_bytes=64)
                 quantise(grouped_of[q], codes_of[q], scales_of[q])
-
-            w = i - 3 - FIRST_WFC
-            if 0 <= w < WFC_PIECES:
-                add_halves(w, tanh_of[w // GROUP_PIECES])
 
             if i < PIECES:
                 scalar_banks = (0, 2) if i >= FIRST_WFC + 2 else (0, 1, 2)
@@ -287,32 +290,39 @@ def tile_dtnnmsg_k_kernel(tc, src_h, he, Wcf_w, Wcf_b, Wdf_w, Wdf_b, Wfc_w, Wfc_
                     raws.append(load_piece(i + RAW_BUFS))
 
             m = i - 2
-            if 0 <= m < FIRST_WFC:
-                c, part = divmod(m, CHUNK_PIECES)
-                if part > 0:
-                    u = part - 1
-                    pair = range(CHUNK_TILES * u, CHUNK_TILES * u + CHUNK_TILES)
-                    if c == 0:
-                        for t in pair:
-                            h_w[t] = sum_pool.tile([P, TOKENS], F32, name="h_w", tag="sum")
-                    hidden_passes(c, u, h_w, codes_of[m], scales_of[m])
-                    if c == CHUNKS - 1:
-                        for t in pair:
-                            hidden_product(t, h_w)
-                if m == FIRST_WFC - 1:
-                    nc.vector.quantize_mx(
-                        out=h_codes[:].bitcast(FP8X4),
-                        scales=h_scales[:],
-                        in_=h_grouped[:].rearrange("p c t -> p (c t)"),
-                    )
-            elif FIRST_WFC <= m < PIECES:
-                w = m - FIRST_WFC
+            w = m - FIRST_WFC
+            if 0 <= w < WFC_PIECES:
                 if w % GROUP_PIECES == 0:
                     tanh_of[w // GROUP_PIECES] = tanh_pool.tile(
                         [P, DEG, GROUP_TILES, NODES], F32, name="tanh_z"
                     )
-                messages(w, codes_of[m], scales_of[m], tanh_of[w // GROUP_PIECES])
+                messages(w, (0, 1), codes_of[m], scales_of[m], tanh_of[w // GROUP_PIECES])
 
-            w = i - 4 - FIRST_WFC
-            if w >= 0 and w % GROUP_PIECES == GROUP_PIECES - 1:
-                sum_and_store(w // GROUP_PIECES, tanh_of[w // GROUP_PIECES])
+            budget = chunk_total * (i + 1) // CHUNK_PIECES - chunk_total * i // CHUNK_PIECES
+            while done < len(passes) and passes[done][0] <= m and (budget > 0 or m == FIRST_WFC - 1):
+                piece, t, s = passes[done]
+                c = piece // CHUNK_PIECES
+                if c == 0 and s == 0:
+                    h_w[t] = sum_pool.tile([P, TOKENS], F32, name="h_w", tag="sum")
+                hidden_pass(c, t, s, h_w, codes_of[piece], scales_of[piece])
+                if c == CHUNKS - 1 and s == CHUNK_PASSES - 1:
+                    hidden_product(t, h_w)
+                done += 1
+                budget -= 1
+            if m == FIRST_WFC - 1:
+                nc.vector.quantize_mx(
+                    out=h_codes[:].bitcast(FP8X4),
+                    scales=h_scales[:],
+                    in_=h_grouped[:].rearrange("p c t -> p (c t)"),
+                )
+
+            g = i - 5 - FIRST_WFC
+            if g >= 0 and g % GROUP_PIECES == GROUP_PIECES - 1:
+                sum_and_store(g // GROUP_PIECES, tanh_of[g // GROUP_PIECES])
+
+            if 0 <= w < WFC_PIECES:
+                messages(w, (2, 3), codes_of[m], scales_of[m], tanh_of[w // GROUP_PIECES])
+
+            a = i - 3 - FIRST_WFC
+            if 0 <= a < WFC_PIECES:
+                add_halves(a, tanh_of[a // GROUP_PIECES])

@@ -52,7 +52,7 @@ def tile_dtnnmsg_k_kernel(tc, src_h, he, Wcf_w, Wcf_b, Wdf_w, Wdf_b, Wfc_w, Wfc_
         grouped_pool = ctx.enter_context(tc.tile_pool(name="grouped", bufs=3))
         codes_pool = ctx.enter_context(tc.tile_pool(name="codes", bufs=4))
         tanh_pool = ctx.enter_context(tc.tile_pool(name="tanh", bufs=3))
-        store_pool = ctx.enter_context(tc.tile_pool(name="store", bufs=2))
+        rows_pool = ctx.enter_context(tc.tile_pool(name="rows", bufs=2))
         flip_pool = ctx.enter_context(tc.psum_pool(name="flip", bufs=4))
         sum_pool = ctx.enter_context(tc.psum_pool(name="sum", bufs=4))
 
@@ -60,8 +60,7 @@ def tile_dtnnmsg_k_kernel(tc, src_h, he, Wcf_w, Wcf_b, Wdf_w, Wdf_b, Wfc_w, Wfc_
         he_rows = he.rearrange("(r x) d b -> (x d) r b", r=TOKEN_TILES)
         wcf_rows = Wcf_w.rearrange("(u p e) a -> u p e a", u=2, e=2)
         wdf_rows = Wdf_w.rearrange("(u p e) b -> p u (e b)", u=2, e=2)
-        wfc_rows = Wfc_w.rearrange("(j p) h -> p j h", p=P)
-        out_tiles = out.rearrange("n (g j p) -> g n j p", j=GROUP_TILES, p=P)
+        wfc_rows = Wfc_w.rearrange("(p j) h -> p j h", j=ATOM_TILES)
 
         def load_piece(i):
             raw = raw_pool.tile([P, PIECE], BF16, tag="raw")
@@ -94,9 +93,8 @@ def tile_dtnnmsg_k_kernel(tc, src_h, he, Wcf_w, Wcf_b, Wdf_w, Wdf_b, Wfc_w, Wfc_
             out=wdf_b_bf[:].rearrange("p (u e) -> p u e", u=2),
             in_=Wdf_b.rearrange("(u p e) -> p u e", u=2, e=2),
         )
-        wfc_b_rows = keep.tile([P, P], BF16)
-        nc.vector.memset(wfc_b_rows[:], 0.0)
-        nc.scalar.dma_start(out=wfc_b_rows[:ATOM_TILES, :], in_=Wfc_b.rearrange("(j p) -> j p", p=P))
+        wfc_b_bf = keep.tile([P, ATOM_TILES], BF16)
+        nc.scalar.dma_start(out=wfc_b_bf[:], in_=Wfc_b.rearrange("(p j) -> p j", j=ATOM_TILES))
 
         raws = [load_piece(i) for i in range(RAW_BUFS)]
 
@@ -149,10 +147,8 @@ def tile_dtnnmsg_k_kernel(tc, src_h, he, Wcf_w, Wcf_b, Wdf_w, Wdf_b, Wfc_w, Wfc_
                 out=e_vw[:, t * TOKENS : (t + 1) * TOKENS], in0=e_sum[:], scalar1=wdf_b[:, t : t + 1]
             )
 
-        wfc_b_flip = flip_pool.tile([P, P], BF16, tag="flip")
-        nc.tensor.transpose(wfc_b_flip[:], wfc_b_rows[:], ident_bf[:])
         wfc_b = keep.tile([P, ATOM_TILES], F32)
-        nc.vector.tensor_copy(out=wfc_b[:], in_=wfc_b_flip[:, :ATOM_TILES])
+        nc.vector.tensor_copy(out=wfc_b[:], in_=wfc_b_bf[:])
 
         src_codes = [
             keep.tile([P, PIECE_CODES], U32, name="src_codes%d" % c, align_bytes=64)
@@ -163,6 +159,7 @@ def tile_dtnnmsg_k_kernel(tc, src_h, he, Wcf_w, Wcf_b, Wdf_w, Wdf_b, Wfc_w, Wfc_
             for c in range(CHUNKS)
         ]
         h_grouped = keep.tile([P, TOKENS, HIDDEN_TILES], BF16, align_bytes=64)
+        sums = keep.tile([P, NODES, ATOM_TILES], F32)
         h_codes = keep.tile([P, TOKENS], U32, align_bytes=64)
         h_scales = keep.tile([P, TOKENS], U8, align_bytes=64)
 
@@ -245,24 +242,32 @@ def tile_dtnnmsg_k_kernel(tc, src_h, he, Wcf_w, Wcf_b, Wdf_w, Wdf_b, Wfc_w, Wfc_
             low = tanh_z[:, :HALF_DEG, first : first + WFC_TILES, :]
             nc.vector.tensor_add(out=low, in0=low, in1=tanh_z[:, HALF_DEG:, first : first + WFC_TILES, :])
 
-        def sum_and_store(group, tanh_z):
+        def sum_halves(tanh_z):
             total = flip_pool.tile([P, P], F32, tag="flip")
-            for dd in range(HALF_DEG):
+            for d in range(HALF_DEG):
                 nc.tensor.matmul(
                     total[:],
-                    lhsT=tanh_z[:, dd, :, :].rearrange("p j n -> p (j n)"),
+                    lhsT=tanh_z[:, d, :, :].rearrange("p j n -> p (j n)"),
                     rhs=ident_f32[:],
                     is_transpose=True,
-                    start=(dd == 0),
-                    stop=(dd == HALF_DEG - 1),
+                    start=(d == 0),
+                    stop=(d == HALF_DEG - 1),
                 )
-            rows = store_pool.tile([P, P], F32, tag="rows")
+            rows = rows_pool.tile([P, P], F32, tag="rows")
             nc.vector.tensor_copy(out=rows[:], in_=total[:])
-            for n in range(NODES):
-                nc.sync.dma_start(out=out_tiles[group, n], in_=rows[n::NODES, :])
+            return rows
+
+        def turn_back(group, rows):
+            back = flip_pool.tile([P, P], F32, tag="flip")
+            nc.tensor.transpose(back[:], rows[:], ident_f32[:])
+            tiles = slice(group * GROUP_TILES, (group + 1) * GROUP_TILES)
+            nc.vector.tensor_copy(
+                out=sums[:, :, tiles].rearrange("p n j -> p j n"),
+                in_=back[:].rearrange("p (j n) -> p j n", n=NODES),
+            )
 
         ctx.enter_context(tc.manual_schedule())
-        grouped_of, codes_of, scales_of, tanh_of, h_w = {}, {}, {}, {}, {}
+        grouped_of, codes_of, scales_of, tanh_of, rows_of, h_w = {}, {}, {}, {}, {}, {}
         passes = [
             (CHUNK_PIECES * c + 1 + t // CHUNK_TILES, t, s)
             for c in range(CHUNKS)
@@ -271,7 +276,7 @@ def tile_dtnnmsg_k_kernel(tc, src_h, he, Wcf_w, Wcf_b, Wdf_w, Wdf_b, Wfc_w, Wfc_
         ]
         chunk_total = HIDDEN_TILES * CHUNK_PASSES
         done = 0
-        for i in range(PIECES + 5):
+        for i in range(PIECES + 6):
             q = i - 1
             if 0 <= q < PIECES:
                 if q < FIRST_WFC and q % CHUNK_PIECES == 0:
@@ -318,7 +323,10 @@ def tile_dtnnmsg_k_kernel(tc, src_h, he, Wcf_w, Wcf_b, Wdf_w, Wdf_b, Wfc_w, Wfc_
 
             g = i - 5 - FIRST_WFC
             if g >= 0 and g % GROUP_PIECES == GROUP_PIECES - 1:
-                sum_and_store(g // GROUP_PIECES, tanh_of[g // GROUP_PIECES])
+                rows_of[g // GROUP_PIECES] = sum_halves(tanh_of[g // GROUP_PIECES])
+            g = i - 6 - FIRST_WFC
+            if g >= 0 and g % GROUP_PIECES == GROUP_PIECES - 1:
+                turn_back(g // GROUP_PIECES, rows_of[g // GROUP_PIECES])
 
             if 0 <= w < WFC_PIECES:
                 messages(w, (2, 3), codes_of[m], scales_of[m], tanh_of[w // GROUP_PIECES])
@@ -326,3 +334,5 @@ def tile_dtnnmsg_k_kernel(tc, src_h, he, Wcf_w, Wcf_b, Wdf_w, Wdf_b, Wfc_w, Wfc_
             a = i - 3 - FIRST_WFC
             if 0 <= a < WFC_PIECES:
                 add_halves(a, tanh_of[a // GROUP_PIECES])
+
+        nc.sync.dma_start(out=out.rearrange("n (p j) -> p n j", j=ATOM_TILES), in_=sums[:])

@@ -52,6 +52,7 @@ def tile_dtnnmsg_k_kernel(tc, src_h, he, Wcf_w, Wcf_b, Wdf_w, Wdf_b, Wfc_w, Wfc_
         grouped_pool = ctx.enter_context(tc.tile_pool(name="grouped", bufs=3))
         codes_pool = ctx.enter_context(tc.tile_pool(name="codes", bufs=4))
         tanh_pool = ctx.enter_context(tc.tile_pool(name="tanh", bufs=3))
+        half_pool = ctx.enter_context(tc.tile_pool(name="half", bufs=3))
         rows_pool = ctx.enter_context(tc.tile_pool(name="rows", bufs=2))
         flip_pool = ctx.enter_context(tc.psum_pool(name="flip", bufs=4))
         sum_pool = ctx.enter_context(tc.psum_pool(name="sum", bufs=4))
@@ -100,6 +101,11 @@ def tile_dtnnmsg_k_kernel(tc, src_h, he, Wcf_w, Wcf_b, Wdf_w, Wdf_b, Wfc_w, Wfc_
 
         ident_f32 = keep.tile([P, P], F32)
         make_identity(nc, ident_f32[:])
+        node_major = keep.tile([P, P], F32)
+        nc.vector.tensor_copy(
+            out=node_major[:].rearrange("p (n j) -> p n j", n=NODES),
+            in_=ident_f32[:].rearrange("p (j n) -> p n j", n=NODES),
+        )
         ident_bf = keep.tile([P, P], BF16)
         make_identity(nc, ident_bf[:])
 
@@ -205,10 +211,10 @@ def tile_dtnnmsg_k_kernel(tc, src_h, he, Wcf_w, Wcf_b, Wdf_w, Wdf_b, Wfc_w, Wfc_
 
         def hidden_product(t, h_w):
             nc.vector.scalar_tensor_tensor(
-                out=h_grouped[:, :, t],
-                in0=h_w[t][:],
+                out=h_grouped[:, :, t].rearrange("p (d n) -> p d n", n=NODES),
+                in0=h_w[t][:].rearrange("p (n d) -> p d n", n=NODES),
                 scalar=wcf_b[:, t : t + 1],
-                in1=e_vw[:, t * TOKENS : (t + 1) * TOKENS],
+                in1=e_vw[:, t * TOKENS : (t + 1) * TOKENS].rearrange("p (n d) -> p d n", n=NODES),
                 op0=add,
                 op1=mult,
             )
@@ -231,23 +237,27 @@ def tile_dtnnmsg_k_kernel(tc, src_h, he, Wcf_w, Wcf_b, Wdf_w, Wdf_b, Wfc_w, Wfc_
                     a = 2 * b + s
                     j = w * WFC_TILES + a
                     nc.scalar.activation(
-                        out=tanh_z[:, :, j % GROUP_TILES, :],
-                        in_=z[:, s * TOKENS : (s + 1) * TOKENS].rearrange("p (n d) -> p d n", n=NODES),
+                        out=tanh_z[:, a, :],
+                        in_=z[:, s * TOKENS : (s + 1) * TOKENS],
                         func=tanh,
                         bias=wfc_b[:, j : j + 1],
                     )
 
-        def add_halves(w, tanh_z):
+        def add_halves(w, tanh_z, half):
             first = (w % GROUP_PIECES) * WFC_TILES
-            low = tanh_z[:, :HALF_DEG, first : first + WFC_TILES, :]
-            nc.vector.tensor_add(out=low, in0=low, in1=tanh_z[:, HALF_DEG:, first : first + WFC_TILES, :])
+            by_neighbour = tanh_z[:].rearrange("p j (d n) -> p d j n", n=NODES)
+            nc.vector.tensor_add(
+                out=half[:, :, first : first + WFC_TILES, :],
+                in0=by_neighbour[:, :HALF_DEG],
+                in1=by_neighbour[:, HALF_DEG:],
+            )
 
-        def sum_halves(tanh_z):
+        def sum_halves(half):
             total = flip_pool.tile([P, P], F32, tag="flip")
             for d in range(HALF_DEG):
                 nc.tensor.matmul(
                     total[:],
-                    lhsT=tanh_z[:, d, :, :].rearrange("p j n -> p (j n)"),
+                    lhsT=half[:, d, :, :].rearrange("p j n -> p (j n)"),
                     rhs=ident_f32[:],
                     is_transpose=True,
                     start=(d == 0),
@@ -259,15 +269,15 @@ def tile_dtnnmsg_k_kernel(tc, src_h, he, Wcf_w, Wcf_b, Wdf_w, Wdf_b, Wfc_w, Wfc_
 
         def turn_back(group, rows):
             back = flip_pool.tile([P, P], F32, tag="flip")
-            nc.tensor.transpose(back[:], rows[:], ident_f32[:])
+            nc.tensor.transpose(back[:], rows[:], node_major[:])
             tiles = slice(group * GROUP_TILES, (group + 1) * GROUP_TILES)
             nc.vector.tensor_copy(
-                out=sums[:, :, tiles].rearrange("p n j -> p j n"),
-                in_=back[:].rearrange("p (j n) -> p j n", n=NODES),
+                out=sums[:, :, tiles], in_=back[:].rearrange("p (n j) -> p n j", n=NODES)
             )
 
         ctx.enter_context(tc.manual_schedule())
-        grouped_of, codes_of, scales_of, tanh_of, rows_of, h_w = {}, {}, {}, {}, {}, {}
+        grouped_of, codes_of, scales_of, h_w = {}, {}, {}, {}
+        tanh_of, half_of, rows_of = {}, {}, {}
         passes = [
             (CHUNK_PIECES * c + 1 + t // CHUNK_TILES, t, s)
             for c in range(CHUNKS)
@@ -297,11 +307,8 @@ def tile_dtnnmsg_k_kernel(tc, src_h, he, Wcf_w, Wcf_b, Wdf_w, Wdf_b, Wfc_w, Wfc_
             m = i - 2
             w = m - FIRST_WFC
             if 0 <= w < WFC_PIECES:
-                if w % GROUP_PIECES == 0:
-                    tanh_of[w // GROUP_PIECES] = tanh_pool.tile(
-                        [P, DEG, GROUP_TILES, NODES], F32, name="tanh_z"
-                    )
-                messages(w, (0, 1), codes_of[m], scales_of[m], tanh_of[w // GROUP_PIECES])
+                tanh_of[w] = tanh_pool.tile([P, WFC_TILES, TOKENS], F32, name="tanh_z")
+                messages(w, (0, 1), codes_of[m], scales_of[m], tanh_of[w])
 
             budget = chunk_total * (i + 1) // CHUNK_PIECES - chunk_total * i // CHUNK_PIECES
             while done < len(passes) and passes[done][0] <= m and (budget > 0 or m == FIRST_WFC - 1):
@@ -323,16 +330,20 @@ def tile_dtnnmsg_k_kernel(tc, src_h, he, Wcf_w, Wcf_b, Wdf_w, Wdf_b, Wfc_w, Wfc_
 
             g = i - 5 - FIRST_WFC
             if g >= 0 and g % GROUP_PIECES == GROUP_PIECES - 1:
-                rows_of[g // GROUP_PIECES] = sum_halves(tanh_of[g // GROUP_PIECES])
+                rows_of[g // GROUP_PIECES] = sum_halves(half_of[g // GROUP_PIECES])
             g = i - 6 - FIRST_WFC
             if g >= 0 and g % GROUP_PIECES == GROUP_PIECES - 1:
                 turn_back(g // GROUP_PIECES, rows_of[g // GROUP_PIECES])
 
             if 0 <= w < WFC_PIECES:
-                messages(w, (2, 3), codes_of[m], scales_of[m], tanh_of[w // GROUP_PIECES])
+                messages(w, (2, 3), codes_of[m], scales_of[m], tanh_of[w])
 
             a = i - 3 - FIRST_WFC
             if 0 <= a < WFC_PIECES:
-                add_halves(a, tanh_of[a // GROUP_PIECES])
+                if a % GROUP_PIECES == 0:
+                    half_of[a // GROUP_PIECES] = half_pool.tile(
+                        [P, HALF_DEG, GROUP_TILES, NODES], F32, name="half"
+                    )
+                add_halves(a, tanh_of[a], half_of[a // GROUP_PIECES])
 
         nc.sync.dma_start(out=out.rearrange("n (p j) -> p n j", j=ATOM_TILES), in_=sums[:])

from contextlib import ExitStack

import concourse.mybir as mybir
from concourse.masks import make_identity

F32 = mybir.dt.float32
BF16 = mybir.dt.bfloat16
U32 = mybir.dt.uint32
U8 = mybir.dt.uint8
FP8X4 = mybir.dt.float8_e4m3fn_x4

P = 128
NODES, DEG, ATOMS, BOND, HIDDEN = 8, 32, 8192, 256, 512
TOKENS = NODES * DEG
TOKEN_TILES = TOKENS // P
HIDDEN_TILES = HIDDEN // P
ATOM_TILES = ATOMS // P
BOND_TILES = BOND // P
K_PASS = 4 * P
PASS_WORDS = K_PASS // 2
BANK = 512

PIECE = 4096
PIECE_WORDS = PIECE // 2
PIECE_BANKS = PIECE_WORDS // BANK
PIECE_CODES = PIECE // 4
CHUNK_TILES = 2
CHUNK_PASSES = PIECE // (CHUNK_TILES * K_PASS)
CHUNK_ATOMS = CHUNK_PASSES * K_PASS
CHUNKS = ATOMS // CHUNK_ATOMS
CHUNK_PIECES = 1 + HIDDEN_TILES // CHUNK_TILES
WFC_TILES = PIECE // HIDDEN
WFC_PIECES = ATOM_TILES // WFC_TILES
FIRST_WFC = CHUNKS * CHUNK_PIECES
PIECES = FIRST_WFC + WFC_PIECES
RAW_BUFS = 11
GROUP_TILES = P // NODES
GROUP_PIECES = GROUP_TILES // WFC_TILES
HALF_DEG = DEG // 2

FLOPS = 2 * TOKENS * (ATOMS * HIDDEN + BOND * HIDDEN + HIDDEN * ATOMS)


def tile_dtnnmsg_k_kernel(tc, src_h, he, Wcf_w, Wcf_b, Wdf_w, Wdf_b, Wfc_w, Wfc_b, out):
    nc = tc.nc
    add, mult = mybir.AluOpType.add, mybir.AluOpType.mult
    tanh = mybir.ActivationFunctionType.Tanh

    with ExitStack() as ctx:
        keep = ctx.enter_context(tc.tile_pool(name="keep", bufs=1))
        raw_pool = ctx.enter_context(tc.tile_pool(name="raw", bufs=RAW_BUFS))
        grouped_pool = ctx.enter_context(tc.tile_pool(name="grouped", bufs=3))
        codes_pool = ctx.enter_context(tc.tile_pool(name="codes", bufs=4))
        tanh_pool = ctx.enter_context(tc.tile_pool(name="tanh", bufs=3))
        half_pool = ctx.enter_context(tc.tile_pool(name="half", bufs=3))
        rows_pool = ctx.enter_context(tc.tile_pool(name="rows", bufs=2))
        flip_pool = ctx.enter_context(tc.psum_pool(name="flip", bufs=4))
        sum_pool = ctx.enter_context(tc.psum_pool(name="sum", bufs=4))

        src_rows = src_h.rearrange("(r x) d a -> (x d) r a", r=TOKEN_TILES)
        he_rows = he.rearrange("(r x) d b -> (x d) r b", r=TOKEN_TILES)
        wcf_rows = Wcf_w.rearrange("(u p e) a -> u p e a", u=2, e=2)
        wdf_rows = Wdf_w.rearrange("(u p e) b -> p u (e b)", u=2, e=2)
        wfc_rows = Wfc_w.rearrange("(p j) h -> p j h", j=ATOM_TILES)

        def load_piece(i):
            raw = raw_pool.tile([P, PIECE], BF16, tag="raw")
            if i < FIRST_WFC:
                c, part = divmod(i, CHUNK_PIECES)
                rows = src_rows if part == 0 else wcf_rows[part - 1]
                nc.sync.dma_start(
                    out=raw[:].rearrange("p (r a) -> p r a", r=CHUNK_TILES),
                    in_=rows[:, :, c * CHUNK_ATOMS : (c + 1) * CHUNK_ATOMS],
                )
            else:
                first = (i - FIRST_WFC) * WFC_TILES
                nc.sync.dma_start(
                    out=raw[:].rearrange("p (j h) -> p j h", j=WFC_TILES),
                    in_=wfc_rows[:, first : first + WFC_TILES, :],
                )
            return raw

        he_sb = keep.tile([P, TOKEN_TILES * BOND], BF16)
        nc.sync.dma_start(out=he_sb[:].rearrange("p (r b) -> p r b", r=TOKEN_TILES), in_=he_rows)
        wdf_sb = keep.tile([P, HIDDEN_TILES * BOND], BF16)
        nc.sync.dma_start(out=wdf_sb[:].rearrange("p (u x) -> p u x", u=2), in_=wdf_rows)
        wcf_b_bf = keep.tile([P, HIDDEN_TILES], BF16)
        nc.scalar.dma_start(
            out=wcf_b_bf[:].rearrange("p (u e) -> p u e", u=2),
            in_=Wcf_b.rearrange("(u p e) -> p u e", u=2, e=2),
        )
        wdf_b_bf = keep.tile([P, HIDDEN_TILES], BF16)
        nc.scalar.dma_start(
            out=wdf_b_bf[:].rearrange("p (u e) -> p u e", u=2),
            in_=Wdf_b.rearrange("(u p e) -> p u e", u=2, e=2),
        )
        wfc_b_bf = keep.tile([P, ATOM_TILES], BF16)
        nc.scalar.dma_start(out=wfc_b_bf[:], in_=Wfc_b.rearrange("(p j) -> p j", j=ATOM_TILES))

        raws = [load_piece(i) for i in range(RAW_BUFS)]

        ident_f32 = keep.tile([P, P], F32)
        make_identity(nc, ident_f32[:])
        node_major = keep.tile([P, P], F32)
        nc.vector.tensor_copy(
            out=node_major[:].rearrange("p (n j) -> p n j", n=NODES),
            in_=ident_f32[:].rearrange("p (j n) -> p n j", n=NODES),
        )
        ident_bf = keep.tile([P, P], BF16)
        make_identity(nc, ident_bf[:])

        warm = keep.tile([P, 2], F32)
        nc.vector.memset(warm[:], 0.0)
        nc.scalar.activation(out=warm[:, 1:2], in_=warm[:, 0:1], func=tanh)

        wcf_b = keep.tile([P, HIDDEN_TILES], F32)
        nc.vector.tensor_copy(out=wcf_b[:], in_=wcf_b_bf[:])
        wdf_b = keep.tile([P, HIDDEN_TILES], F32)
        nc.vector.tensor_copy(out=wdf_b[:], in_=wdf_b_bf[:])

        wdf_flip = flip_pool.tile([P, BOND_TILES * HIDDEN], BF16, tag="flip")
        for kb in range(BOND_TILES):
            for t in range(HIDDEN_TILES):
                nc.tensor.transpose(
                    wdf_flip[:, (kb * HIDDEN_TILES + t) * P : (kb * HIDDEN_TILES + t + 1) * P],
                    wdf_sb[:, t * BOND + kb * P : t * BOND + (kb + 1) * P],
                    ident_bf[:],
                )
        wdf_t = keep.tile([P, BOND_TILES * HIDDEN], BF16)
        nc.vector.tensor_copy(out=wdf_t[:], in_=wdf_flip[:])
        he_flip = flip_pool.tile([P, BOND_TILES * TOKENS], BF16, tag="flip")
        for kb in range(BOND_TILES):
            for r in range(TOKEN_TILES):
                nc.tensor.transpose(
                    he_flip[:, (kb * TOKEN_TILES + r) * P : (kb * TOKEN_TILES + r + 1) * P],
                    he_sb[:, r * BOND + kb * P : r * BOND + (kb + 1) * P],
                    ident_bf[:],
                )
        he_t = keep.tile([P, BOND_TILES * TOKENS], BF16)
        nc.scalar.copy(out=he_t[:], in_=he_flip[:])
        e_vw = keep.tile([P, HIDDEN_TILES * TOKENS], F32)
        for t in range(HIDDEN_TILES):
            e_sum = sum_pool.tile([P, TOKENS], F32, tag="sum")
            for kb in range(BOND_TILES):
                nc.tensor.matmul(
                    e_sum[:],
                    lhsT=wdf_t[:, (kb * HIDDEN_TILES + t) * P : (kb * HIDDEN_TILES + t + 1) * P],
                    rhs=he_t[:, kb * TOKENS : (kb + 1) * TOKENS],
                    start=(kb == 0),
                    stop=(kb == BOND_TILES - 1),
                )
            nc.vector.tensor_scalar_add(
                out=e_vw[:, t * TOKENS : (t + 1) * TOKENS], in0=e_sum[:], scalar1=wdf_b[:, t : t + 1]
            )

        wfc_b = keep.tile([P, ATOM_TILES], F32)
        nc.vector.tensor_copy(out=wfc_b[:], in_=wfc_b_bf[:])

        src_codes = [
            keep.tile([P, PIECE_CODES], U32, name="src_codes%d" % c, align_bytes=64)
            for c in range(CHUNKS)
        ]
        src_scales = [
            keep.tile([P, PIECE_CODES], U8, name="src_scales%d" % c, align_bytes=64)
            for c in range(CHUNKS)
        ]
        h_grouped = keep.tile([P, TOKENS, HIDDEN_TILES], BF16, align_bytes=64)
        sums = keep.tile([P, NODES, ATOM_TILES], F32)
        h_codes = keep.tile([P, TOKENS], U32, align_bytes=64)
        h_scales = keep.tile([P, TOKENS], U8, align_bytes=64)

        def transpose_and_regroup(raw, row_tiles, scalar_banks):
            bank_passes = BANK // (2 * P * row_tiles)
            words = raw[:].bitcast(F32).rearrange("p (r g u w) -> p r g u w", r=row_tiles, u=2, w=P)
            grouped = grouped_pool.tile([P, PIECE], BF16, tag="grouped", align_bytes=64)
            grouped_words = grouped[:].bitcast(F32)
            for b in range(PIECE_BANKS):
                flip = flip_pool.tile([P, BANK], F32, tag="flip")
                blocks = flip[:].rearrange("p (g u r w) -> p g u r w", g=bank_passes, u=2, r=row_tiles)
                for g in range(bank_passes):
                    for u in range(2):
                        for r in range(row_tiles):
                            nc.tensor.transpose(
                                blocks[:, g, u, r, :], words[:, r, b * bank_passes + g, u, :], ident_f32[:]
                            )
                pairs_in = flip[:].rearrange("p (g u c) -> p g c u", g=bank_passes, u=2)
                pairs_out = grouped_words[:, b * BANK : (b + 1) * BANK].rearrange(
                    "p (g c u) -> p g c u", g=bank_passes, u=2
                )
                if b in scalar_banks:
                    nc.scalar.copy(out=pairs_out, in_=pairs_in)
                else:
                    nc.vector.tensor_copy(out=pairs_out, in_=pairs_in)
            return grouped

        def quantise(grouped, codes, scales):
            nc.vector.quantize_mx(out=codes[:].bitcast(FP8X4), scales=scales[:], in_=grouped[:])

        def hidden_pass(c, t, s, h_w, codes, scales):
            first_row = (CHUNK_TILES * s + t % CHUNK_TILES) * P
            rows = slice(first_row, first_row + P)
            nc.tensor.matmul_mx(
                out=h_w[t][:],
                lhsT=codes[:, rows].bitcast(FP8X4),
                lhsT_scale=scales[:, rows],
                rhs=src_codes[c][:, s * TOKENS : (s + 1) * TOKENS].bitcast(FP8X4),
                rhs_scale=src_scales[c][:, s * TOKENS : (s + 1) * TOKENS],
                start=(c == 0 and s == 0),
                stop=(c == CHUNKS - 1 and s == CHUNK_PASSES - 1),
            )

        def hidden_product(t, h_w):
            nc.vector.scalar_tensor_tensor(
                out=h_grouped[:, :, t].rearrange("p (d n) -> p d n", n=NODES),
                in0=h_w[t][:].rearrange("p (n d) -> p d n", n=NODES),
                scalar=wcf_b[:, t : t + 1],
                in1=e_vw[:, t * TOKENS : (t + 1) * TOKENS].rearrange("p (n d) -> p d n", n=NODES),
                op0=add,
                op1=mult,
            )

        def messages(w, banks, codes, scales, tanh_z):
            for b in banks:
                z = sum_pool.tile([P, 2 * TOKENS], F32, tag="sum")
                for s in range(2):
                    a = 2 * b + s
                    nc.tensor.matmul_mx(
                        out=z[:, s * TOKENS : (s + 1) * TOKENS],
                        lhsT=codes[:, a * P : (a + 1) * P].bitcast(FP8X4),
                        lhsT_scale=scales[:, a * P : (a + 1) * P],
                        rhs=h_codes[:].bitcast(FP8X4),
                        rhs_scale=h_scales[:],
                        start=True,
                        stop=True,
                    )
                for s in range(2):
                    a = 2 * b + s
                    j = w * WFC_TILES + a
                    nc.scalar.activation(
                        out=tanh_z[:, a, :],
                        in_=z[:, s * TOKENS : (s + 1) * TOKENS],
                        func=tanh,
                        bias=wfc_b[:, j : j + 1],
                    )

        def add_halves(w, tanh_z, half):
            first = (w % GROUP_PIECES) * WFC_TILES
            by_neighbour = tanh_z[:].rearrange("p j (d n) -> p d j n", n=NODES)
            nc.vector.tensor_add(
                out=half[:, :, first : first + WFC_TILES, :],
                in0=by_neighbour[:, :HALF_DEG],
                in1=by_neighbour[:, HALF_DEG:],
            )

        def sum_halves(half):
            total = flip_pool.tile([P, P], F32, tag="flip")
            for d in range(HALF_DEG):
                nc.tensor.matmul(
                    total[:],
                    lhsT=half[:, d, :, :].rearrange("p j n -> p (j n)"),
                    rhs=ident_f32[:],
                    is_transpose=True,
                    start=(d == 0),
                    stop=(d == HALF_DEG - 1),
                )
            rows = rows_pool.tile([P, P], F32, tag="rows")
            nc.vector.tensor_copy(out=rows[:], in_=total[:])
            return rows

        def turn_back(group, rows):
            back = flip_pool.tile([P, P], F32, tag="flip")
            nc.tensor.transpose(back[:], rows[:], node_major[:])
            tiles = slice(group * GROUP_TILES, (group + 1) * GROUP_TILES)
            nc.vector.tensor_copy(
                out=sums[:, :, tiles], in_=back[:].rearrange("p (n j) -> p n j", n=NODES)
            )

        ctx.enter_context(tc.manual_schedule())
        grouped_of, codes_of, scales_of, h_w = {}, {}, {}, {}
        tanh_of, half_of, rows_of = {}, {}, {}
        passes = [
            (CHUNK_PIECES * c + 1 + t // CHUNK_TILES, t, s)
            for c in range(CHUNKS)
            for t in range(HIDDEN_TILES)
            for s in range(CHUNK_PASSES)
        ]
        chunk_total = HIDDEN_TILES * CHUNK_PASSES
        done = 0
        for i in range(PIECES + 6):
            q = i - 1
            if 0 <= q < PIECES:
                if q < FIRST_WFC and q % CHUNK_PIECES == 0:
                    codes_of[q], scales_of[q] = src_codes[q // CHUNK_PIECES], src_scales[q // CHUNK_PIECES]
                else:
                    codes_of[q] = codes_pool.tile([P, PIECE_CODES], U32, name="codes", align_bytes=64)
                    scales_of[q] = codes_pool.tile([P, PIECE_CODES], U8, name="scales", align_bytes=64)
                quantise(grouped_of[q], codes_of[q], scales_of[q])

            if i < PIECES:
                scalar_banks = (0, 2) if i >= FIRST_WFC + 2 else (0, 1, 2)
                grouped_of[i] = transpose_and_regroup(
                    raws[i], CHUNK_TILES if i < FIRST_WFC else 1, scalar_banks
                )
                if i + RAW_BUFS < PIECES:
                    raws.append(load_piece(i + RAW_BUFS))

            m = i - 2
            w = m - FIRST_WFC
            if 0 <= w < WFC_PIECES:
                tanh_of[w] = tanh_pool.tile([P, WFC_TILES, TOKENS], F32, name="tanh_z")
                messages(w, (0, 1), codes_of[m], scales_of[m], tanh_of[w])

            budget = chunk_total * (i + 1) // CHUNK_PIECES - chunk_total * i // CHUNK_PIECES
            while done < len(passes) and passes[done][0] <= m and (budget > 0 or m == FIRST_WFC - 1):
                piece, t, s = passes[done]
                c = piece // CHUNK_PIECES
                if c == 0 and s == 0:
                    h_w[t] = sum_pool.tile([P, TOKENS], F32, name="h_w", tag="sum")
                hidden_pass(c, t, s, h_w, codes_of[piece], scales_of[piece])
                if c == CHUNKS - 1 and s == CHUNK_PASSES - 1:
                    hidden_product(t, h_w)
                done += 1
                budget -= 1
            if m == FIRST_WFC - 1:
                nc.vector.quantize_mx(
                    out=h_codes[:].bitcast(FP8X4),
                    scales=h_scales[:],
                    in_=h_grouped[:].rearrange("p c t -> p (c t)"),
                )

            g = i - 5 - FIRST_WFC
            if g >= 0 and g % GROUP_PIECES == GROUP_PIECES - 1:
                rows_of[g // GROUP_PIECES] = sum_halves(half_of[g // GROUP_PIECES])
            g = i - 6 - FIRST_WFC
            if g >= 0 and g % GROUP_PIECES == GROUP_PIECES - 1:
                turn_back(g // GROUP_PIECES, rows_of[g // GROUP_PIECES])

            if 0 <= w < WFC_PIECES:
                messages(w, (2, 3), codes_of[m], scales_of[m], tanh_of[w])

            a = i - 3 - FIRST_WFC
            if 0 <= a < WFC_PIECES:
                if a % GROUP_PIECES == 0:
                    half_of[a // GROUP_PIECES] = half_pool.tile(
                        [P, HALF_DEG, GROUP_TILES, NODES], F32, name="half"
                    )
                add_halves(a, tanh_of[a], half_of[a // GROUP_PIECES])

        nc.sync.dma_start(out=out.rearrange("n (p j) -> p n j", j=ATOM_TILES), in_=sums[:])
